import numpy as np
import ml_dtypes


def mxq(x, axis, fmt="e4m3"):
    dtype, down = {"e4m3": (ml_dtypes.float8_e4m3fn, 7), "e5m2": (ml_dtypes.float8_e5m2, 14)}[fmt]
    v = np.moveaxis(np.asarray(x, np.float32).astype(ml_dtypes.bfloat16).astype(np.float64), axis, -1)
    blocks = v.reshape(v.shape[:-1] + (-1, 32))
    amax = np.abs(blocks).max(-1, keepdims=True)
    byte = np.maximum(np.where(amax > 0, np.frexp(amax)[1] - 1 + 127, 0) - down, 1)
    scale = np.exp2(byte - 127.0)
    codes = (blocks / scale).astype(np.float32).astype(dtype).astype(np.float64)
    return np.moveaxis((codes * scale).reshape(v.shape), -1, axis)


WIDE = False


def mx_kscale(k):
    if not WIDE:
        return np.ones(k)
    levels = np.array([10, -10, 5, -5, 0])
    a = np.random.permutation(np.resize(levels, k // 512 * 4)).reshape(k // 512, 4)
    idx = np.arange(k)
    return np.exp2(a[idx // 512, idx % 128 // 32])


BF16 = ml_dtypes.bfloat16


def bf(x):
    return np.asarray(x, np.float32).astype(BF16)


def f64(x):
    return np.asarray(x).astype(np.float64)


B, H, P, D, NF, DO, G = 2, 12, 32, 512, 8, 512, 5
N = D * H * P


def setup_inputs():
    s = mx_kscale(D)
    return {
        "x": bf(np.random.standard_normal((B, H, P, D)) * s),
        "lin_w": bf(np.random.standard_normal((G * D, D)) * 0.3 / np.sqrt(D) / s),
        "lin_b": bf(np.random.standard_normal(G * D) * 0.1),
        "grid": bf(np.arange(NF)[None, :] + 1.0 + 0.1 * np.random.standard_normal((G, NF))),
        "coef": bf(np.random.standard_normal((N, NF, G)) * 0.5),
        "shift": bf(np.random.standard_normal((1, H, G, P, D)) * 0.5),
    }


def reference(x, lin_w, lin_b, grid, coef, shift):
    xl = (mxq(f64(x), 3, "e4m3") @ mxq(f64(lin_w).T, 0, "e4m3")) + f64(lin_b)
    xl = xl.reshape(B, G, N)
    sn = np.sin(f64(grid)[None, :, :, None] * xl[:, :, None, :])
    f = sn * f64(coef).transpose(2, 1, 0)[None]
    return f.reshape(B, H, G, NF, P, D).sum(axis=3) + f64(shift)

@@ -1,0 +1,227 @@
+import math
+from contextlib import ExitStack
+
+import concourse.mybir as mybir
+from concourse.masks import make_identity
+
+F32 = mybir.dt.float32
+BF16 = mybir.dt.bfloat16
+I32 = mybir.dt.int32
+U32 = mybir.dt.uint32
+U8 = mybir.dt.uint8
+FP8X4 = mybir.dt.float8_e4m3fn_x4
+ALU = mybir.AluOpType
+ACT = mybir.ActivationFunctionType
+
+P = 128
+BATCH = 2
+X_ROWS = 384
+K = 512
+W_BLOCKS = 20
+GROUPS = 5
+FREQS = 8
+SEG = 128
+TILES = 12
+UNIT_TILES = 4
+UNITS = TILES // UNIT_TILES
+UNIT = UNIT_TILES * SEG
+WINDOW = 128
+WINDOW_STEP = 64
+ROWS = 78
+TERMS = 8
+
+FLOPS = 2 * BATCH * X_ROWS * K * W_BLOCKS * P
+
+
+def tile_ka_attention_heads_mod_pa_kernel(tc, x, lin_w, lin_b, grid, coef, shift, out):
+    nc = tc.nc
+
+    x_view = x.rearrange("b h p k -> (b h p) k").rearrange("(a p) k -> p a k", p=P)
+    w_view = lin_w.rearrange("(a p) k -> p a k", p=P)
+    coef_view = coef.rearrange("(t q d) m j -> t q (d m j)", q=P, d=SEG)
+    shift_view = shift.rearrange("o h g p (c d) -> (p c) (o h g) d", d=SEG)
+    out_view = out.rearrange("b h g p (c d) -> (p c) b (h g) d", d=SEG)
+
+    with ExitStack() as stack:
+        keep = stack.enter_context(tc.tile_pool(name="keep", bufs=1))
+        psum_units = stack.enter_context(tc.psum_pool(name="psum_units", bufs=2 * UNITS))
+        psum_work = stack.enter_context(tc.psum_pool(name="psum_work", bufs=2))
+
+        x_tiles = BATCH * X_ROWS // P
+        x_codes = keep.tile([P, x_tiles * P], U32, name="x_codes", align_bytes=64)
+        x_scales = keep.tile([P, x_tiles * P], U8, name="x_scales", align_bytes=64)
+        w_codes = keep.tile([P, W_BLOCKS * P], U32, name="w_codes", align_bytes=64)
+        w_scales = keep.tile([P, W_BLOCKS * P], U8, name="w_scales", align_bytes=64)
+        coef_sb = keep.tile([P, TILES * SEG, FREQS * GROUPS], BF16, name="coef_sb")
+        shift_sb = keep.tile([P, GROUPS * TILES, SEG], BF16, name="shift_sb")
+        ident = keep.tile([P, P], F32, name="ident")
+        bias_t = keep.tile([P, W_BLOCKS], F32, name="bias_t")
+        turns = keep.tile([P, GROUPS * FREQS], F32, name="turns")
+
+        with tc.tile_pool(name="prep", bufs=1) as prep:
+            x_raw = prep.tile([P, x_tiles * K], BF16, name="x_raw")
+            w_raw = prep.tile([P, W_BLOCKS * K], BF16, name="w_raw")
+            x_grouped = prep.tile([P, x_tiles * P * 4], BF16, name="x_grouped", align_bytes=64)
+            w_grouped = prep.tile([P, W_BLOCKS * P * 4], BF16, name="w_grouped", align_bytes=64)
+            bias_rows = prep.tile([P, P], BF16, name="bias_rows")
+            bias_rows_f = prep.tile([P, P], F32, name="bias_rows_f")
+            grid_bc = prep.tile([P, GROUPS * FREQS], BF16, name="grid_bc")
+
+            nc.vector.memset(bias_rows[:], 0.0)
+            make_identity(nc, ident[:])
+
+            nc.sync.dma_start(out=x_raw[:].rearrange("p (a k) -> p a k", k=K), in_=x_view)
+            for c in range(GROUPS):
+                nc.sync.dma_start(
+                    out=w_raw[:, c * 4 * K : (c + 1) * 4 * K].rearrange("p (a k) -> p a k", k=K),
+                    in_=w_view[:, c * 4 : (c + 1) * 4, :],
+                )
+            for t in range(TILES):
+                nc.sync.dma_start(
+                    out=coef_sb[:, t * SEG : (t + 1) * SEG, :].rearrange("p d c -> p (d c)"),
+                    in_=coef_view[t],
+                )
+            nc.scalar.dma_start(out=bias_rows[0:W_BLOCKS, :], in_=lin_b.rearrange("(a d) -> a d", d=P))
+            nc.scalar.dma_start(out=grid_bc[:], in_=grid.rearrange("j m -> (j m)").partition_broadcast(P))
+            nc.scalar.dma_start(out=shift_sb[:], in_=shift_view)
+
+            nc.vector.tensor_scalar(
+                out=turns[:], in0=grid_bc[:], scalar1=1.0 / (2.0 * math.pi), scalar2=None, op0=ALU.mult
+            )
+
+            nc.vector.tensor_copy(out=bias_rows_f[:], in_=bias_rows[:])
+            bias_ps = psum_work.tile([P, UNIT], F32, name="bias_ps", tag="work")
+            nc.tensor.transpose(bias_ps[:, 0:P], bias_rows_f[:], ident[:])
+            nc.vector.tensor_copy(out=bias_t[:], in_=bias_ps[:, 0:W_BLOCKS])
+
+            def put_k_on_partitions(raw, grouped, n_tiles):
+                words = raw[:].bitcast(F32)
+                grouped_words = grouped[:].bitcast(F32)
+                for pair in range(n_tiles // 2):
+                    bank = psum_units.tile([P, UNIT], F32, name="turned", tag="bank")
+                    for a in range(2):
+                        for u in range(2):
+                            first = ((pair * 2 + a) * 2 + u) * P
+                            nc.tensor.transpose(
+                                bank[:, (a * 2 + u) * P : (a * 2 + u + 1) * P],
+                                words[:, first : first + P],
+                                ident[:],
+                            )
+                    dst = grouped_words[:, pair * UNIT : (pair + 1) * UNIT].rearrange(
+                        "p (a r u) -> p a r u", a=2, u=2
+                    )
+                    src = bank[:].rearrange("p (a u r) -> p a r u", a=2, u=2)
+                    if pair % 2 == 0:
+                        nc.vector.tensor_copy(out=dst, in_=src)
+                    else:
+                        nc.scalar.copy(out=dst, in_=src)
+
+            def quantise(grouped, codes, scales, n_rows):
+                for first in range(0, n_rows, 512):
+                    n = min(512, n_rows - first)
+                    nc.vector.quantize_mx(
+                        out=codes[:, first : first + n].bitcast(FP8X4),
+                        scales=scales[:, first : first + n],
+                        in_=grouped[:, first * 4 : (first + n) * 4],
+                    )
+
+            put_k_on_partitions(x_raw, x_grouped, x_tiles)
+            put_k_on_partitions(w_raw, w_grouped, W_BLOCKS)
+            quantise(x_grouped, x_codes, x_scales, x_tiles * P)
+            quantise(w_grouped, w_codes, w_scales, W_BLOCKS * P)
+
+        loop = stack.enter_context(tc.tile_pool(name="loop", bufs=2))
+
+        def project(j):
+            first_row = min((2 * SEG * j) // W_BLOCKS, WINDOW - ROWS)
+            xl_t = loop.tile([P, BATCH, ROWS * W_BLOCKS], F32, name="xl_t", tag="xl_t", bufs=1)
+            for b in range(BATCH):
+                window = b * X_ROWS + WINDOW_STEP * j
+                for c in range(GROUPS):
+                    acc = psum_work.tile([P, UNIT], F32, name="acc", tag="work")
+                    for d in range(4):
+                        a = c * 4 + d
+                        nc.tensor.matmul_mx(
+                            out=acc[:, d * WINDOW : (d + 1) * WINDOW],
+                            lhsT=w_codes[:, a * P : (a + 1) * P].bitcast(FP8X4),
+                            lhsT_scale=w_scales[:, a * P : (a + 1) * P],
+                            rhs=x_codes[:, window : window + WINDOW].bitcast(FP8X4),
+                            rhs_scale=x_scales[:, window : window + WINDOW],
+                            start=True,
+                            stop=True,
+                        )
+                    nc.vector.tensor_tensor(
+                        out=xl_t[:, b, :].rearrange("p (r a) -> p r a", a=W_BLOCKS)[:, :, c * 4 : (c + 1) * 4],
+                        in0=acc[:].rearrange("p (d r) -> p r d", d=4)[:, first_row : first_row + ROWS, :],
+                        in1=bias_t[:, c * 4 : (c + 1) * 4].unsqueeze(1).to_broadcast([P, ROWS, 4]),
+                        op=ALU.add,
+                    )
+            return xl_t, 2 * SEG * j - W_BLOCKS * first_row
+
+        def turn(xl_t, first_seg, unit):
+            x_sb = loop.tile([P, BATCH, UNIT], F32, name="x_sb", tag="x_sb", bufs=UNITS)
+            x_ps = []
+            for b in range(BATCH):
+                bank = psum_units.tile([P, UNIT], F32, name="x_ps", tag="bank")
+                for t in range(UNIT_TILES):
+                    seg = first_seg + SEG * (unit * UNIT_TILES + t)
+                    nc.tensor.transpose(bank[:, t * SEG : (t + 1) * SEG], xl_t[:, b, seg : seg + P], ident[:])
+                nc.scalar.copy(out=x_sb[:, b, :], in_=bank[:])
+                x_ps.append(bank)
+            return x_ps, x_sb
+
+        xl_t, first_seg = project(0)
+        units = [turn(xl_t, first_seg, unit) for unit in range(UNITS)]
+        terms = None
+        for j in range(GROUPS):
+            for m in range(FREQS):
+                for unit in range(UNITS):
+                    x_ps, x_sb = units[unit]
+                    block, half = divmod((j * FREQS + m) * UNITS + unit, 2)
+                    rate = turns[:, j * FREQS + m : j * FREQS + m + 1]
+
+                    whole = loop.tile([P, BATCH, UNIT], I32, name="whole")
+                    nc.vector.tensor_scalar(out=whole[:], in0=x_sb[:], scalar1=rate, scalar2=None, op0=ALU.mult)
+                    frac = loop.tile([P, BATCH, UNIT], F32, name="frac")
+                    for b in range(BATCH):
+                        nc.vector.scalar_tensor_tensor(
+                            out=frac[:, b, :],
+                            in0=x_ps[b][:],
+                            scalar=rate,
+                            in1=whole[:, b, :],
+                            op0=ALU.mult,
+                            op1=ALU.subtract,
+                        )
+                    sine = loop.tile([P, BATCH, UNIT], F32, name="sine")
+                    nc.scalar.activation(out=sine[:], in_=frac[:], func=ACT.Sin, scale=2.0 * math.pi)
+
+                    if half == 0:
+                        terms = loop.tile([P, BATCH, (TERMS + 1) * SEG], F32, name="terms")
+                        nc.scalar.copy(
+                            out=terms[:, :, TERMS * SEG :],
+                            in_=shift_sb[:, block : block + 1, :].to_broadcast([P, BATCH, SEG]),
+                        )
+                    column = m * GROUPS + j
+                    nc.gpsimd.tensor_tensor(
+                        out=terms[:, :, half * UNIT : (half + 1) * UNIT],
+                        in0=sine[:],
+                        in1=coef_sb[:, unit * UNIT : (unit + 1) * UNIT, column : column + 1]
+                        .rearrange("p n c -> p c n")
+                        .to_broadcast([P, BATCH, UNIT]),
+                        op=ALU.mult,
+                    )
+                    if half == 1:
+                        total = loop.tile([P, BATCH, SEG], F32, name="total")
+                        nc.vector.tensor_reduce(
+                            out=total[:],
+                            in_=terms[:].rearrange("p b (e d) -> p b d e", d=SEG),
+                            axis=mybir.AxisListType.X,
+                            op=ALU.add,
+                        )
+                        nc.sync.dma_start(out=out_view[:, :, block, :], in_=total[:])
+
+                    if j + 1 < GROUPS:
+                        if m == 0 and unit == UNITS - 1:
+                            xl_t, first_seg = project(j + 1)
+                        if m == FREQS - 1:
+                            units[unit] = turn(xl_t, first_seg, unit)

@@ -29,6 +29,7 @@ WINDOW = 128
 WINDOW_STEP = 64
 ROWS = 78
 TERMS = 8
+LAG = 3
 
 FLOPS = 2 * BATCH * X_ROWS * K * W_BLOCKS * P
 
@@ -170,58 +171,70 @@ def tile_ka_attention_heads_mod_pa_kernel(tc, x, lin_w, lin_b, grid, coef, shift
                 x_ps.append(bank)
             return x_ps, x_sb
 
-        xl_t, first_seg = project(0)
-        units = [turn(xl_t, first_seg, unit) for unit in range(UNITS)]
-        terms = None
-        for j in range(GROUPS):
-            for m in range(FREQS):
-                for unit in range(UNITS):
-                    x_ps, x_sb = units[unit]
-                    block, half = divmod((j * FREQS + m) * UNITS + unit, 2)
-                    rate = turns[:, j * FREQS + m : j * FREQS + m + 1]
+        def start_half(i, x_ps, x_sb):
+            jm, unit = divmod(i, UNITS)
+            j, m = divmod(jm, FREQS)
+            block, half = divmod(i, 2)
+            rate = turns[:, jm : jm + 1]
 
-                    whole = loop.tile([P, BATCH, UNIT], I32, name="whole")
-                    nc.vector.tensor_scalar(out=whole[:], in0=x_sb[:], scalar1=rate, scalar2=None, op0=ALU.mult)
-                    frac = loop.tile([P, BATCH, UNIT], F32, name="frac")
-                    for b in range(BATCH):
-                        nc.vector.scalar_tensor_tensor(
-                            out=frac[:, b, :],
-                            in0=x_ps[b][:],
-                            scalar=rate,
-                            in1=whole[:, b, :],
-                            op0=ALU.mult,
-                            op1=ALU.subtract,
-                        )
-                    sine = loop.tile([P, BATCH, UNIT], F32, name="sine")
-                    nc.scalar.activation(out=sine[:], in_=frac[:], func=ACT.Sin, scale=2.0 * math.pi)
+            whole = loop.tile([P, BATCH, UNIT], I32, name="whole")
+            nc.vector.tensor_scalar(out=whole[:], in0=x_sb[:], scalar1=rate, scalar2=None, op0=ALU.mult)
+            frac = loop.tile([P, BATCH, UNIT], F32, name="frac")
+            for b in range(BATCH):
+                nc.vector.scalar_tensor_tensor(
+                    out=frac[:, b, :],
+                    in0=x_ps[b][:],
+                    scalar=rate,
+                    in1=whole[:, b, :],
+                    op0=ALU.mult,
+                    op1=ALU.subtract,
+                )
+            sine = loop.tile([P, BATCH, UNIT], F32, name="sine")
+            nc.scalar.activation(out=sine[:], in_=frac[:], func=ACT.Sin, scale=2.0 * math.pi)
 
-                    if half == 0:
-                        terms = loop.tile([P, BATCH, (TERMS + 1) * SEG], F32, name="terms")
-                        nc.scalar.copy(
-                            out=terms[:, :, TERMS * SEG :],
-                            in_=shift_sb[:, block : block + 1, :].to_broadcast([P, BATCH, SEG]),
-                        )
-                    column = m * GROUPS + j
-                    nc.gpsimd.tensor_tensor(
-                        out=terms[:, :, half * UNIT : (half + 1) * UNIT],
-                        in0=sine[:],
-                        in1=coef_sb[:, unit * UNIT : (unit + 1) * UNIT, column : column + 1]
-                        .rearrange("p n c -> p c n")
-                        .to_broadcast([P, BATCH, UNIT]),
-                        op=ALU.mult,
-                    )
-                    if half == 1:
-                        total = loop.tile([P, BATCH, SEG], F32, name="total")
-                        nc.vector.tensor_reduce(
-                            out=total[:],
-                            in_=terms[:].rearrange("p b (e d) -> p b d e", d=SEG),
-                            axis=mybir.AxisListType.X,
-                            op=ALU.add,
-                        )
-                        nc.sync.dma_start(out=out_view[:, :, block, :], in_=total[:])
+            if half == 0:
+                terms_of[block] = loop.tile([P, BATCH, (TERMS + 1) * SEG], F32, name="terms", bufs=3)
+                nc.scalar.copy(
+                    out=terms_of[block][:, :, TERMS * SEG :],
+                    in_=shift_sb[:, block : block + 1, :].to_broadcast([P, BATCH, SEG]),
+                )
+            column = m * GROUPS + j
+            nc.gpsimd.tensor_tensor(
+                out=terms_of[block][:, :, half * UNIT : (half + 1) * UNIT],
+                in0=sine[:],
+                in1=coef_sb[:, unit * UNIT : (unit + 1) * UNIT, column : column + 1]
+                .rearrange("p n c -> p c n")
+                .to_broadcast([P, BATCH, UNIT]),
+                op=ALU.mult,
+            )
 
+        def finish_block(block):
+            total = loop.tile([P, BATCH, SEG], F32, name="total")
+            nc.vector.tensor_reduce(
+                out=total[:],
+                in_=terms_of[block][:].rearrange("p b (e d) -> p b d e", d=SEG),
+                axis=mybir.AxisListType.X,
+                op=ALU.add,
+            )
+            nc.sync.dma_start(out=out_view[:, :, block, :], in_=total[:])
+
+        halves = GROUPS * FREQS * UNITS
+        halves_per_group = FREQS * UNITS
+        terms_of = {}
+        with tc.manual_schedule():
+            xl_t, first_seg = project(0)
+            units = [turn(xl_t, first_seg, unit) for unit in range(UNITS)]
+            for i in range(halves + LAG):
+                if i < halves:
+                    x_ps, x_sb = units[i % UNITS]
+                    start_half(i, x_ps, x_sb)
+                    j, local = divmod(i, halves_per_group)
                     if j + 1 < GROUPS:
-                        if m == 0 and unit == UNITS - 1:
+                        if local == UNITS:
                             xl_t, first_seg = project(j + 1)
-                        if m == FREQS - 1:
-                            units[unit] = turn(xl_t, first_seg, unit)
+                        if local > halves_per_group - UNITS:
+                            units[(i - 1) % UNITS] = turn(xl_t, first_seg, (i - 1) % UNITS)
+                    if j > 0 and local == 0:
+                        units[UNITS - 1] = turn(xl_t, first_seg, UNITS - 1)
+                if i >= LAG and (i - LAG) % 2 == 1:
+                    finish_block((i - LAG) // 2)

@@ -29,7 +29,6 @@ WINDOW = 128
 WINDOW_STEP = 64
 ROWS = 78
 TERMS = 8
-LAG = 3
 
 FLOPS = 2 * BATCH * X_ROWS * K * W_BLOCKS * P
 
@@ -58,6 +57,8 @@ def tile_ka_attention_heads_mod_pa_kernel(tc, x, lin_w, lin_b, grid, coef, shift
         ident = keep.tile([P, P], F32, name="ident")
         bias_t = keep.tile([P, W_BLOCKS], F32, name="bias_t")
         turns = keep.tile([P, GROUPS * FREQS], F32, name="turns")
+        minus_quarter = keep.tile([P, 1], F32, name="minus_quarter")
+        quarter_turn = keep.tile([P, 1], F32, name="quarter_turn")
 
         with tc.tile_pool(name="prep", bufs=1) as prep:
             x_raw = prep.tile([P, x_tiles * K], BF16, name="x_raw")
@@ -69,6 +70,10 @@ def tile_ka_attention_heads_mod_pa_kernel(tc, x, lin_w, lin_b, grid, coef, shift
             grid_bc = prep.tile([P, GROUPS * FREQS], BF16, name="grid_bc")
 
             nc.vector.memset(bias_rows[:], 0.0)
+            nc.vector.memset(minus_quarter[:], -0.25)
+            nc.vector.tensor_scalar(
+                out=quarter_turn[:], in0=minus_quarter[:], scalar1=-2.0 * math.pi, scalar2=None, op0=ALU.mult
+            )
             make_identity(nc, ident[:])
 
             nc.sync.dma_start(out=x_raw[:].rearrange("p (a k) -> p a k", k=K), in_=x_view)
@@ -171,35 +176,43 @@ def tile_ka_attention_heads_mod_pa_kernel(tc, x, lin_w, lin_b, grid, coef, shift
                 x_ps.append(bank)
             return x_ps, x_sb
 
-        def start_half(i, x_ps, x_sb):
+        def sines(i):
             jm, unit = divmod(i, UNITS)
-            j, m = divmod(jm, FREQS)
-            block, half = divmod(i, 2)
+            x_ps, x_sb = units[unit]
             rate = turns[:, jm : jm + 1]
-
             whole = loop.tile([P, BATCH, UNIT], I32, name="whole")
-            nc.vector.tensor_scalar(out=whole[:], in0=x_sb[:], scalar1=rate, scalar2=None, op0=ALU.mult)
-            frac = loop.tile([P, BATCH, UNIT], F32, name="frac")
+            nc.vector.tensor_scalar(
+                out=whole[:], in0=x_sb[:], scalar1=rate, scalar2=-0.25, op0=ALU.mult, op1=ALU.add
+            )
+            rest = loop.tile([P, BATCH, UNIT], F32, name="rest")
             for b in range(BATCH):
                 nc.vector.scalar_tensor_tensor(
-                    out=frac[:, b, :],
+                    out=rest[:, b, :],
                     in0=x_ps[b][:],
                     scalar=rate,
                     in1=whole[:, b, :],
                     op0=ALU.mult,
                     op1=ALU.subtract,
                 )
+            nc.scalar.activation(out=rest[:], in_=rest[:], func=ACT.Abs, bias=minus_quarter[:, 0:1])
             sine = loop.tile([P, BATCH, UNIT], F32, name="sine")
-            nc.scalar.activation(out=sine[:], in_=frac[:], func=ACT.Sin, scale=2.0 * math.pi)
+            nc.scalar.activation(
+                out=sine[:], in_=rest[:], func=ACT.Sin, scale=-2.0 * math.pi, bias=quarter_turn[:, 0:1]
+            )
+            return sine
 
+        def four_terms(i, sine):
+            jm, unit = divmod(i, UNITS)
+            j, m = divmod(jm, FREQS)
+            block, half = divmod(i, 2)
             if half == 0:
-                terms_of[block] = loop.tile([P, BATCH, (TERMS + 1) * SEG], F32, name="terms", bufs=3)
+                terms_of[block] = loop.tile([P, BATCH, (TERMS + 1) * SEG], F32, name="terms")
                 nc.scalar.copy(
                     out=terms_of[block][:, :, TERMS * SEG :],
                     in_=shift_sb[:, block : block + 1, :].to_broadcast([P, BATCH, SEG]),
                 )
             column = m * GROUPS + j
-            nc.gpsimd.tensor_tensor(
+            nc.vector.tensor_tensor(
                 out=terms_of[block][:, :, half * UNIT : (half + 1) * UNIT],
                 in0=sine[:],
                 in1=coef_sb[:, unit * UNIT : (unit + 1) * UNIT, column : column + 1]
@@ -221,20 +234,20 @@ def tile_ka_attention_heads_mod_pa_kernel(tc, x, lin_w, lin_b, grid, coef, shift
         halves = GROUPS * FREQS * UNITS
         halves_per_group = FREQS * UNITS
         terms_of = {}
+        sine_of = {}
         with tc.manual_schedule():
             xl_t, first_seg = project(0)
             units = [turn(xl_t, first_seg, unit) for unit in range(UNITS)]
-            for i in range(halves + LAG):
+            for i in range(halves + 1):
                 if i < halves:
-                    x_ps, x_sb = units[i % UNITS]
-                    start_half(i, x_ps, x_sb)
-                    j, local = divmod(i, halves_per_group)
-                    if j + 1 < GROUPS:
-                        if local == UNITS:
-                            xl_t, first_seg = project(j + 1)
-                        if local > halves_per_group - UNITS:
-                            units[(i - 1) % UNITS] = turn(xl_t, first_seg, (i - 1) % UNITS)
-                    if j > 0 and local == 0:
-                        units[UNITS - 1] = turn(xl_t, first_seg, UNITS - 1)
-                if i >= LAG and (i - LAG) % 2 == 1:
-                    finish_block((i - LAG) // 2)
+                    sine_of[i] = sines(i)
+                if i >= 1:
+                    four_terms(i - 1, sine_of[i - 1])
+                    if (i - 1) % 2 == 1:
+                        finish_block((i - 1) // 2)
+                j, local = divmod(i, halves_per_group)
+                if j + 1 < GROUPS and local == UNITS:
+                    xl_t, first_seg = project(j + 1)
+                last_used = i - 1
+                if i >= 1 and last_used % halves_per_group >= halves_per_group - UNITS and last_used + UNITS < halves:
+                    units[last_used % UNITS] = turn(xl_t, first_seg, last_used % UNITS)

@@ -44,8 +44,9 @@ def tile_ka_attention_heads_mod_pa_kernel(tc, x, lin_w, lin_b, grid, coef, shift
 
     with ExitStack() as stack:
         keep = stack.enter_context(tc.tile_pool(name="keep", bufs=1))
-        psum_units = stack.enter_context(tc.psum_pool(name="psum_units", bufs=2 * UNITS))
-        psum_work = stack.enter_context(tc.psum_pool(name="psum_work", bufs=2))
+        psum_turn = stack.enter_context(tc.psum_pool(name="psum_turn", bufs=4))
+        psum_acc = stack.enter_context(tc.psum_pool(name="psum_acc", bufs=2))
+        psum_sums = stack.enter_context(tc.psum_pool(name="psum_sums", bufs=2))
 
         x_tiles = BATCH * X_ROWS // P
         x_codes = keep.tile([P, x_tiles * P], U32, name="x_codes", align_bytes=64)
@@ -96,7 +97,7 @@ def tile_ka_attention_heads_mod_pa_kernel(tc, x, lin_w, lin_b, grid, coef, shift
             )
 
             nc.vector.tensor_copy(out=bias_rows_f[:], in_=bias_rows[:])
-            bias_ps = psum_work.tile([P, UNIT], F32, name="bias_ps", tag="work")
+            bias_ps = psum_acc.tile([P, UNIT], F32, name="bias_ps", tag="acc")
             nc.tensor.transpose(bias_ps[:, 0:P], bias_rows_f[:], ident[:])
             nc.vector.tensor_copy(out=bias_t[:], in_=bias_ps[:, 0:W_BLOCKS])
 
@@ -104,7 +105,7 @@ def tile_ka_attention_heads_mod_pa_kernel(tc, x, lin_w, lin_b, grid, coef, shift
                 words = raw[:].bitcast(F32)
                 grouped_words = grouped[:].bitcast(F32)
                 for pair in range(n_tiles // 2):
-                    bank = psum_units.tile([P, UNIT], F32, name="turned", tag="bank")
+                    bank = psum_turn.tile([P, UNIT], F32, name="turned", tag="bank")
                     for a in range(2):
                         for u in range(2):
                             first = ((pair * 2 + a) * 2 + u) * P
@@ -140,11 +141,12 @@ def tile_ka_attention_heads_mod_pa_kernel(tc, x, lin_w, lin_b, grid, coef, shift
 
         def project(j):
             first_row = min((2 * SEG * j) // W_BLOCKS, WINDOW - ROWS)
-            xl_t = loop.tile([P, BATCH, ROWS * W_BLOCKS], F32, name="xl_t", tag="xl_t", bufs=1)
+            first_seg = 2 * SEG * j - W_BLOCKS * first_row
+            xl_t = loop.tile([P, BATCH, ROWS * W_BLOCKS], F32, name="xl_t", bufs=1)
             for b in range(BATCH):
                 window = b * X_ROWS + WINDOW_STEP * j
                 for c in range(GROUPS):
-                    acc = psum_work.tile([P, UNIT], F32, name="acc", tag="work")
+                    acc = psum_acc.tile([P, UNIT], F32, name="acc", tag="acc")
                     for d in range(4):
                         a = c * 4 + d
                         nc.tensor.matmul_mx(
@@ -162,38 +164,28 @@ def tile_ka_attention_heads_mod_pa_kernel(tc, x, lin_w, lin_b, grid, coef, shift
                         in1=bias_t[:, c * 4 : (c + 1) * 4].unsqueeze(1).to_broadcast([P, ROWS, 4]),
                         op=ALU.add,
                     )
-            return xl_t, 2 * SEG * j - W_BLOCKS * first_row
+            units = []
+            for unit in range(UNITS):
+                xl = loop.tile([P, BATCH, UNIT], F32, name="xl", bufs=2 * UNITS)
+                for b in range(BATCH):
+                    bank = psum_turn.tile([P, UNIT], F32, name="xl_ps", tag="bank")
+                    for t in range(UNIT_TILES):
+                        seg = first_seg + SEG * (unit * UNIT_TILES + t)
+                        nc.tensor.transpose(bank[:, t * SEG : (t + 1) * SEG], xl_t[:, b, seg : seg + P], ident[:])
+                    nc.scalar.copy(out=xl[:, b, :], in_=bank[:])
+                units.append(xl)
+            return units
 
-        def turn(xl_t, first_seg, unit):
-            x_sb = loop.tile([P, BATCH, UNIT], F32, name="x_sb", tag="x_sb", bufs=UNITS)
-            x_ps = []
-            for b in range(BATCH):
-                bank = psum_units.tile([P, UNIT], F32, name="x_ps", tag="bank")
-                for t in range(UNIT_TILES):
-                    seg = first_seg + SEG * (unit * UNIT_TILES + t)
-                    nc.tensor.transpose(bank[:, t * SEG : (t + 1) * SEG], xl_t[:, b, seg : seg + P], ident[:])
-                nc.scalar.copy(out=x_sb[:, b, :], in_=bank[:])
-                x_ps.append(bank)
-            return x_ps, x_sb
-
-        def sines(i):
-            jm, unit = divmod(i, UNITS)
-            x_ps, x_sb = units[unit]
-            rate = turns[:, jm : jm + 1]
-            whole = loop.tile([P, BATCH, UNIT], I32, name="whole")
+        def sines(i, xl):
+            rate = turns[:, i // UNITS : i // UNITS + 1]
+            whole = loop.tile([P, BATCH, UNIT], I32, name="whole", bufs=1)
             nc.vector.tensor_scalar(
-                out=whole[:], in0=x_sb[:], scalar1=rate, scalar2=-0.25, op0=ALU.mult, op1=ALU.add
+                out=whole[:], in0=xl[:], scalar1=rate, scalar2=-0.25, op0=ALU.mult, op1=ALU.add
             )
             rest = loop.tile([P, BATCH, UNIT], F32, name="rest")
-            for b in range(BATCH):
-                nc.vector.scalar_tensor_tensor(
-                    out=rest[:, b, :],
-                    in0=x_ps[b][:],
-                    scalar=rate,
-                    in1=whole[:, b, :],
-                    op0=ALU.mult,
-                    op1=ALU.subtract,
-                )
+            nc.vector.scalar_tensor_tensor(
+                out=rest[:], in0=xl[:], scalar=rate, in1=whole[:], op0=ALU.mult, op1=ALU.subtract
+            )
             nc.scalar.activation(out=rest[:], in_=rest[:], func=ACT.Abs, bias=minus_quarter[:, 0:1])
             sine = loop.tile([P, BATCH, UNIT], F32, name="sine")
             nc.scalar.activation(
@@ -204,50 +196,68 @@ def tile_ka_attention_heads_mod_pa_kernel(tc, x, lin_w, lin_b, grid, coef, shift
         def four_terms(i, sine):
             jm, unit = divmod(i, UNITS)
             j, m = divmod(jm, FREQS)
-            block, half = divmod(i, 2)
-            if half == 0:
-                terms_of[block] = loop.tile([P, BATCH, (TERMS + 1) * SEG], F32, name="terms")
-                nc.scalar.copy(
-                    out=terms_of[block][:, :, TERMS * SEG :],
-                    in_=shift_sb[:, block : block + 1, :].to_broadcast([P, BATCH, SEG]),
-                )
             column = m * GROUPS + j
-            nc.vector.tensor_tensor(
-                out=terms_of[block][:, :, half * UNIT : (half + 1) * UNIT],
+            products = loop.tile([P, BATCH, UNIT], F32, name="products", bufs=4)
+            nc.gpsimd.tensor_tensor(
+                out=products[:],
                 in0=sine[:],
                 in1=coef_sb[:, unit * UNIT : (unit + 1) * UNIT, column : column + 1]
                 .rearrange("p n c -> p c n")
                 .to_broadcast([P, BATCH, UNIT]),
                 op=ALU.mult,
             )
+            return products
 
-        def finish_block(block):
+        def add_up(block):
+            shift_f = loop.tile([P, SEG], F32, name="shift_f")
+            nc.scalar.copy(out=shift_f[:], in_=shift_sb[:, block, :])
+            sums = psum_sums.tile([P, UNIT], F32, name="sums")
+            for b in range(BATCH):
+                cells = sums[:, b * SEG : (b + 1) * SEG]
+                for e in range(TERMS):
+                    products = products_of[2 * block + e // UNIT_TILES]
+                    t = e % UNIT_TILES
+                    nc.tensor.matmul(
+                        out=cells,
+                        lhsT=products[:, b, t * SEG : (t + 1) * SEG],
+                        rhs=ident[:],
+                        is_transpose=True,
+                        start=(e == 0),
+                        stop=False,
+                    )
+                nc.tensor.matmul(out=cells, lhsT=shift_f[:], rhs=ident[:], is_transpose=True, start=False, stop=True)
+            sums_of[block] = sums
+
+        def turn_back(block):
+            sums = sums_of[block]
+            sums_sb = loop.tile([P, BATCH * SEG], F32, name="sums_sb")
+            nc.scalar.copy(out=sums_sb[:], in_=sums[:, 0 : BATCH * SEG])
+            for b in range(BATCH):
+                nc.tensor.transpose(
+                    sums[:, (BATCH + b) * SEG : (BATCH + b + 1) * SEG], sums_sb[:, b * SEG : (b + 1) * SEG], ident[:]
+                )
+
+        def store(block):
             total = loop.tile([P, BATCH, SEG], F32, name="total")
-            nc.vector.tensor_reduce(
-                out=total[:],
-                in_=terms_of[block][:].rearrange("p b (e d) -> p b d e", d=SEG),
-                axis=mybir.AxisListType.X,
-                op=ALU.add,
-            )
+            nc.scalar.copy(out=total[:].rearrange("p b d -> p (b d)"), in_=sums_of[block][:, BATCH * SEG :])
             nc.sync.dma_start(out=out_view[:, :, block, :], in_=total[:])
 
         halves = GROUPS * FREQS * UNITS
         halves_per_group = FREQS * UNITS
-        terms_of = {}
         sine_of = {}
+        products_of = {}
+        sums_of = {}
         with tc.manual_schedule():
-            xl_t, first_seg = project(0)
-            units = [turn(xl_t, first_seg, unit) for unit in range(UNITS)]
-            for i in range(halves + 1):
-                if i < halves:
-                    sine_of[i] = sines(i)
-                if i >= 1:
-                    four_terms(i - 1, sine_of[i - 1])
-                    if (i - 1) % 2 == 1:
-                        finish_block((i - 1) // 2)
+            units_of = {0: project(0)}
+            for i in range(halves + 4):
                 j, local = divmod(i, halves_per_group)
-                if j + 1 < GROUPS and local == UNITS:
-                    xl_t, first_seg = project(j + 1)
-                last_used = i - 1
-                if i >= 1 and last_used % halves_per_group >= halves_per_group - UNITS and last_used + UNITS < halves:
-                    units[last_used % UNITS] = turn(xl_t, first_seg, last_used % UNITS)
+                if i < halves:
+                    sine_of[i] = sines(i, units_of[j][i % UNITS])
+                if 1 <= i <= halves:
+                    products_of[i - 1] = four_terms(i - 1, sine_of[i - 1])
+                for stage, action in enumerate((add_up, turn_back, store)):
+                    block, odd = divmod(i - 1 - stage, 2)
+                    if odd == 1 and 0 <= block < halves // 2:
+                        action(block)
+                if j + 1 < GROUPS and local == halves_per_group // 2:
+                    units_of[j + 1] = project(j + 1)

@@ -29,6 +29,7 @@ WINDOW = 128
 WINDOW_STEP = 64
 ROWS = 78
 TERMS = 8
+COEF_AHEAD = 2
 
 FLOPS = 2 * BATCH * X_ROWS * K * W_BLOCKS * P
 
@@ -44,7 +45,7 @@ def tile_ka_attention_heads_mod_pa_kernel(tc, x, lin_w, lin_b, grid, coef, shift
 
     with ExitStack() as stack:
         keep = stack.enter_context(tc.tile_pool(name="keep", bufs=1))
-        psum_turn = stack.enter_context(tc.psum_pool(name="psum_turn", bufs=4))
+        psum_turn = stack.enter_context(tc.psum_pool(name="psum_turn", bufs=3))
         psum_acc = stack.enter_context(tc.psum_pool(name="psum_acc", bufs=2))
         psum_sums = stack.enter_context(tc.psum_pool(name="psum_sums", bufs=2))
 
@@ -56,6 +57,7 @@ def tile_ka_attention_heads_mod_pa_kernel(tc, x, lin_w, lin_b, grid, coef, shift
         coef_sb = keep.tile([P, TILES * SEG, FREQS * GROUPS], BF16, name="coef_sb")
         shift_sb = keep.tile([P, GROUPS * TILES, SEG], BF16, name="shift_sb")
         ident = keep.tile([P, P], F32, name="ident")
+        ident_bf = keep.tile([P, P], BF16, name="ident_bf")
         bias_t = keep.tile([P, W_BLOCKS], F32, name="bias_t")
         turns = keep.tile([P, GROUPS * FREQS], F32, name="turns")
         minus_quarter = keep.tile([P, 1], F32, name="minus_quarter")
@@ -76,6 +78,7 @@ def tile_ka_attention_heads_mod_pa_kernel(tc, x, lin_w, lin_b, grid, coef, shift
                 out=quarter_turn[:], in0=minus_quarter[:], scalar1=-2.0 * math.pi, scalar2=None, op0=ALU.mult
             )
             make_identity(nc, ident[:])
+            make_identity(nc, ident_bf[:])
 
             nc.sync.dma_start(out=x_raw[:].rearrange("p (a k) -> p a k", k=K), in_=x_view)
             for c in range(GROUPS):
@@ -141,8 +144,7 @@ def tile_ka_attention_heads_mod_pa_kernel(tc, x, lin_w, lin_b, grid, coef, shift
 
         def project(j):
             first_row = min((2 * SEG * j) // W_BLOCKS, WINDOW - ROWS)
-            first_seg = 2 * SEG * j - W_BLOCKS * first_row
-            xl_t = loop.tile([P, BATCH, ROWS * W_BLOCKS], F32, name="xl_t", bufs=1)
+            xl_t = loop.tile([P, BATCH, ROWS * W_BLOCKS], F32, name="xl_t")
             for b in range(BATCH):
                 window = b * X_ROWS + WINDOW_STEP * j
                 for c in range(GROUPS):
@@ -164,27 +166,31 @@ def tile_ka_attention_heads_mod_pa_kernel(tc, x, lin_w, lin_b, grid, coef, shift
                         in1=bias_t[:, c * 4 : (c + 1) * 4].unsqueeze(1).to_broadcast([P, ROWS, 4]),
                         op=ALU.add,
                     )
-            units = []
-            for unit in range(UNITS):
-                xl = loop.tile([P, BATCH, UNIT], F32, name="xl", bufs=2 * UNITS)
-                for b in range(BATCH):
-                    bank = psum_turn.tile([P, UNIT], F32, name="xl_ps", tag="bank")
-                    for t in range(UNIT_TILES):
-                        seg = first_seg + SEG * (unit * UNIT_TILES + t)
-                        nc.tensor.transpose(bank[:, t * SEG : (t + 1) * SEG], xl_t[:, b, seg : seg + P], ident[:])
-                    nc.scalar.copy(out=xl[:, b, :], in_=bank[:])
-                units.append(xl)
-            return units
+            return xl_t, 2 * SEG * j - W_BLOCKS * first_row
 
-        def sines(i, xl):
-            rate = turns[:, i // UNITS : i // UNITS + 1]
+        def turn_coef(i):
+            jm, unit = divmod(i, UNITS)
+            j, m = divmod(jm, FREQS)
+            column = m * GROUPS + j
+            turned = psum_turn.tile([P, UNIT], BF16, name="coef_ps", tag="bank")
+            for t in range(UNIT_TILES):
+                first = (unit * UNIT_TILES + t) * SEG
+                nc.tensor.transpose(
+                    turned[:, t * SEG : (t + 1) * SEG], coef_sb[:, first : first + SEG, column], ident_bf[:]
+                )
+            coef_t = loop.tile([P, UNIT], BF16, name="coef_t", bufs=6)
+            nc.vector.tensor_copy(out=coef_t[:], in_=turned[:])
+            return coef_t
+
+        def sines(i, xl_t, first_seg):
+            jm, unit = divmod(i, UNITS)
+            rate = turns[:, jm : jm + 1]
+            xl = xl_t[:, :, first_seg + unit * UNIT : first_seg + (unit + 1) * UNIT]
             whole = loop.tile([P, BATCH, UNIT], I32, name="whole", bufs=1)
-            nc.vector.tensor_scalar(
-                out=whole[:], in0=xl[:], scalar1=rate, scalar2=-0.25, op0=ALU.mult, op1=ALU.add
-            )
+            nc.vector.tensor_scalar(out=whole[:], in0=xl, scalar1=rate, scalar2=-0.25, op0=ALU.mult, op1=ALU.add)
             rest = loop.tile([P, BATCH, UNIT], F32, name="rest")
             nc.vector.scalar_tensor_tensor(
-                out=rest[:], in0=xl[:], scalar=rate, in1=whole[:], op0=ALU.mult, op1=ALU.subtract
+                out=rest[:], in0=xl, scalar=rate, in1=whole[:], op0=ALU.mult, op1=ALU.subtract
             )
             nc.scalar.activation(out=rest[:], in_=rest[:], func=ACT.Abs, bias=minus_quarter[:, 0:1])
             sine = loop.tile([P, BATCH, UNIT], F32, name="sine")
@@ -193,71 +199,64 @@ def tile_ka_attention_heads_mod_pa_kernel(tc, x, lin_w, lin_b, grid, coef, shift
             )
             return sine
 
-        def four_terms(i, sine):
-            jm, unit = divmod(i, UNITS)
-            j, m = divmod(jm, FREQS)
-            column = m * GROUPS + j
-            products = loop.tile([P, BATCH, UNIT], F32, name="products", bufs=4)
+        def four_terms(sine, coef_t):
+            products = loop.tile([P, BATCH, UNIT], F32, name="products", bufs=6)
             nc.gpsimd.tensor_tensor(
                 out=products[:],
                 in0=sine[:],
-                in1=coef_sb[:, unit * UNIT : (unit + 1) * UNIT, column : column + 1]
-                .rearrange("p n c -> p c n")
-                .to_broadcast([P, BATCH, UNIT]),
+                in1=coef_t[:].unsqueeze(1).to_broadcast([P, BATCH, UNIT]),
                 op=ALU.mult,
             )
             return products
 
         def add_up(block):
-            shift_f = loop.tile([P, SEG], F32, name="shift_f")
-            nc.scalar.copy(out=shift_f[:], in_=shift_sb[:, block, :])
-            sums = psum_sums.tile([P, UNIT], F32, name="sums")
+            sums = psum_sums.tile([P, BATCH, SEG], F32, name="sums")
             for b in range(BATCH):
-                cells = sums[:, b * SEG : (b + 1) * SEG]
                 for e in range(TERMS):
                     products = products_of[2 * block + e // UNIT_TILES]
                     t = e % UNIT_TILES
                     nc.tensor.matmul(
-                        out=cells,
+                        out=sums[:, b, :],
                         lhsT=products[:, b, t * SEG : (t + 1) * SEG],
                         rhs=ident[:],
                         is_transpose=True,
                         start=(e == 0),
-                        stop=False,
+                        stop=(e == TERMS - 1),
                     )
-                nc.tensor.matmul(out=cells, lhsT=shift_f[:], rhs=ident[:], is_transpose=True, start=False, stop=True)
             sums_of[block] = sums
-
-        def turn_back(block):
-            sums = sums_of[block]
-            sums_sb = loop.tile([P, BATCH * SEG], F32, name="sums_sb")
-            nc.scalar.copy(out=sums_sb[:], in_=sums[:, 0 : BATCH * SEG])
-            for b in range(BATCH):
-                nc.tensor.transpose(
-                    sums[:, (BATCH + b) * SEG : (BATCH + b + 1) * SEG], sums_sb[:, b * SEG : (b + 1) * SEG], ident[:]
-                )
 
         def store(block):
             total = loop.tile([P, BATCH, SEG], F32, name="total")
-            nc.scalar.copy(out=total[:].rearrange("p b d -> p (b d)"), in_=sums_of[block][:, BATCH * SEG :])
+            nc.vector.tensor_tensor(
+                out=total[:],
+                in0=sums_of[block][:],
+                in1=shift_sb[:, block : block + 1, :].to_broadcast([P, BATCH, SEG]),
+                op=ALU.add,
+            )
             nc.sync.dma_start(out=out_view[:, :, block, :], in_=total[:])
 
         halves = GROUPS * FREQS * UNITS
         halves_per_group = FREQS * UNITS
+        coef_t_of = {}
         sine_of = {}
         products_of = {}
         sums_of = {}
         with tc.manual_schedule():
-            units_of = {0: project(0)}
-            for i in range(halves + 4):
+            xl_of = {0: project(0)}
+            for i in range(COEF_AHEAD):
+                coef_t_of[i] = turn_coef(i)
+            for i in range(halves + 5):
                 j, local = divmod(i, halves_per_group)
                 if i < halves:
-                    sine_of[i] = sines(i, units_of[j][i % UNITS])
+                    xl_t, first_seg = xl_of[j]
+                    sine_of[i] = sines(i, xl_t, first_seg)
+                if i + COEF_AHEAD < halves:
+                    coef_t_of[i + COEF_AHEAD] = turn_coef(i + COEF_AHEAD)
                 if 1 <= i <= halves:
-                    products_of[i - 1] = four_terms(i - 1, sine_of[i - 1])
-                for stage, action in enumerate((add_up, turn_back, store)):
-                    block, odd = divmod(i - 1 - stage, 2)
-                    if odd == 1 and 0 <= block < halves // 2:
-                        action(block)
+                    products_of[i - 1] = four_terms(sine_of[i - 1], coef_t_of[i - 1])
+                if i >= 3 and i % 2 == 1 and (i - 3) // 2 < halves // 2:
+                    add_up((i - 3) // 2)
+                if i >= 5 and i % 2 == 1:
+                    store((i - 5) // 2)
                 if j + 1 < GROUPS and local == halves_per_group // 2:
-                    units_of[j + 1] = project(j + 1)
+                    xl_of[j + 1] = project(j + 1)

@@ -29,7 +29,7 @@ WINDOW = 128
 WINDOW_STEP = 64
 ROWS = 78
 TERMS = 8
-COEF_AHEAD = 2
+COEF_AHEAD = 4
 
 FLOPS = 2 * BATCH * X_ROWS * K * W_BLOCKS * P
 
@@ -55,7 +55,6 @@ def tile_ka_attention_heads_mod_pa_kernel(tc, x, lin_w, lin_b, grid, coef, shift
         w_codes = keep.tile([P, W_BLOCKS * P], U32, name="w_codes", align_bytes=64)
         w_scales = keep.tile([P, W_BLOCKS * P], U8, name="w_scales", align_bytes=64)
         coef_sb = keep.tile([P, TILES * SEG, FREQS * GROUPS], BF16, name="coef_sb")
-        shift_sb = keep.tile([P, GROUPS * TILES, SEG], BF16, name="shift_sb")
         ident = keep.tile([P, P], F32, name="ident")
         ident_bf = keep.tile([P, P], BF16, name="ident_bf")
         bias_t = keep.tile([P, W_BLOCKS], F32, name="bias_t")
@@ -93,7 +92,6 @@ def tile_ka_attention_heads_mod_pa_kernel(tc, x, lin_w, lin_b, grid, coef, shift
                 )
             nc.scalar.dma_start(out=bias_rows[0:W_BLOCKS, :], in_=lin_b.rearrange("(a d) -> a d", d=P))
             nc.scalar.dma_start(out=grid_bc[:], in_=grid.rearrange("j m -> (j m)").partition_broadcast(P))
-            nc.scalar.dma_start(out=shift_sb[:], in_=shift_view)
 
             nc.vector.tensor_scalar(
                 out=turns[:], in0=grid_bc[:], scalar1=1.0 / (2.0 * math.pi), scalar2=None, op0=ALU.mult
@@ -144,6 +142,8 @@ def tile_ka_attention_heads_mod_pa_kernel(tc, x, lin_w, lin_b, grid, coef, shift
 
         def project(j):
             first_row = min((2 * SEG * j) // W_BLOCKS, WINDOW - ROWS)
+            shift_sb = loop.tile([P, TILES, SEG], BF16, name="shift_sb")
+            nc.sync.dma_start(out=shift_sb[:], in_=shift_view[:, j * TILES : (j + 1) * TILES, :])
             xl_t = loop.tile([P, BATCH, ROWS * W_BLOCKS], F32, name="xl_t")
             for b in range(BATCH):
                 window = b * X_ROWS + WINDOW_STEP * j
@@ -166,7 +166,7 @@ def tile_ka_attention_heads_mod_pa_kernel(tc, x, lin_w, lin_b, grid, coef, shift
                         in1=bias_t[:, c * 4 : (c + 1) * 4].unsqueeze(1).to_broadcast([P, ROWS, 4]),
                         op=ALU.add,
                     )
-            return xl_t, 2 * SEG * j - W_BLOCKS * first_row
+            return xl_t, 2 * SEG * j - W_BLOCKS * first_row, shift_sb
 
         def turn_coef(i):
             jm, unit = divmod(i, UNITS)
@@ -178,8 +178,11 @@ def tile_ka_attention_heads_mod_pa_kernel(tc, x, lin_w, lin_b, grid, coef, shift
                 nc.tensor.transpose(
                     turned[:, t * SEG : (t + 1) * SEG], coef_sb[:, first : first + SEG, column], ident_bf[:]
                 )
-            coef_t = loop.tile([P, UNIT], BF16, name="coef_t", bufs=6)
-            nc.vector.tensor_copy(out=coef_t[:], in_=turned[:])
+            return turned
+
+        def keep_coef(turned):
+            coef_t = loop.tile([P, UNIT], BF16, name="coef_t", bufs=COEF_AHEAD + 2)
+            nc.scalar.copy(out=coef_t[:], in_=turned[:])
             return coef_t
 
         def sines(i, xl_t, first_seg):
@@ -188,20 +191,20 @@ def tile_ka_attention_heads_mod_pa_kernel(tc, x, lin_w, lin_b, grid, coef, shift
             xl = xl_t[:, :, first_seg + unit * UNIT : first_seg + (unit + 1) * UNIT]
             whole = loop.tile([P, BATCH, UNIT], I32, name="whole", bufs=1)
             nc.vector.tensor_scalar(out=whole[:], in0=xl, scalar1=rate, scalar2=-0.25, op0=ALU.mult, op1=ALU.add)
-            rest = loop.tile([P, BATCH, UNIT], F32, name="rest")
+            rest = loop.tile([P, BATCH, UNIT], F32, name="rest", bufs=3)
             nc.vector.scalar_tensor_tensor(
                 out=rest[:], in0=xl, scalar=rate, in1=whole[:], op0=ALU.mult, op1=ALU.subtract
             )
             nc.scalar.activation(out=rest[:], in_=rest[:], func=ACT.Abs, bias=minus_quarter[:, 0:1])
-            sine = loop.tile([P, BATCH, UNIT], F32, name="sine")
+            sine = loop.tile([P, BATCH, UNIT], F32, name="sine", bufs=3)
             nc.scalar.activation(
                 out=sine[:], in_=rest[:], func=ACT.Sin, scale=-2.0 * math.pi, bias=quarter_turn[:, 0:1]
             )
             return sine
 
         def four_terms(sine, coef_t):
-            products = loop.tile([P, BATCH, UNIT], F32, name="products", bufs=6)
-            nc.gpsimd.tensor_tensor(
+            products = loop.tile([P, BATCH, UNIT], F32, name="products", bufs=5)
+            nc.vector.tensor_tensor(
                 out=products[:],
                 in0=sine[:],
                 in1=coef_t[:].unsqueeze(1).to_broadcast([P, BATCH, UNIT]),
@@ -230,13 +233,14 @@ def tile_ka_attention_heads_mod_pa_kernel(tc, x, lin_w, lin_b, grid, coef, shift
             nc.vector.tensor_tensor(
                 out=total[:],
                 in0=sums_of[block][:],
-                in1=shift_sb[:, block : block + 1, :].to_broadcast([P, BATCH, SEG]),
+                in1=xl_of[block // TILES][2][:, block % TILES : block % TILES + 1, :].to_broadcast([P, BATCH, SEG]),
                 op=ALU.add,
             )
             nc.sync.dma_start(out=out_view[:, :, block, :], in_=total[:])
 
         halves = GROUPS * FREQS * UNITS
         halves_per_group = FREQS * UNITS
+        turned_of = {}
         coef_t_of = {}
         sine_of = {}
         products_of = {}
@@ -244,19 +248,23 @@ def tile_ka_attention_heads_mod_pa_kernel(tc, x, lin_w, lin_b, grid, coef, shift
         with tc.manual_schedule():
             xl_of = {0: project(0)}
             for i in range(COEF_AHEAD):
-                coef_t_of[i] = turn_coef(i)
-            for i in range(halves + 5):
+                turned_of[i] = turn_coef(i)
+                if i >= 1:
+                    coef_t_of[i - 1] = keep_coef(turned_of[i - 1])
+            for i in range(halves + 3):
                 j, local = divmod(i, halves_per_group)
                 if i < halves:
-                    xl_t, first_seg = xl_of[j]
-                    sine_of[i] = sines(i, xl_t, first_seg)
-                if i + COEF_AHEAD < halves:
-                    coef_t_of[i + COEF_AHEAD] = turn_coef(i + COEF_AHEAD)
+                    sine_of[i] = sines(i, xl_of[j][0], xl_of[j][1])
+                ahead = i + COEF_AHEAD
+                if ahead < halves:
+                    turned_of[ahead] = turn_coef(ahead)
+                if ahead - 1 < halves:
+                    coef_t_of[ahead - 1] = keep_coef(turned_of[ahead - 1])
                 if 1 <= i <= halves:
                     products_of[i - 1] = four_terms(sine_of[i - 1], coef_t_of[i - 1])
-                if i >= 3 and i % 2 == 1 and (i - 3) // 2 < halves // 2:
-                    add_up((i - 3) // 2)
-                if i >= 5 and i % 2 == 1:
-                    store((i - 5) // 2)
+                if i >= 2 and i % 2 == 0 and i <= halves:
+                    add_up((i - 2) // 2)
+                if i >= 3 and i % 2 == 1:
+                    store((i - 3) // 2)
                 if j + 1 < GROUPS and local == halves_per_group // 2:
                     xl_of[j + 1] = project(j + 1)

@@ -29,7 +29,9 @@ WINDOW = 128
 WINDOW_STEP = 64
 ROWS = 78
 TERMS = 8
-COEF_AHEAD = 4
+WHOLE_AHEAD = 2
+PRODUCT_LAG = 2
+STORE_LAG = 2
 
 FLOPS = 2 * BATCH * X_ROWS * K * W_BLOCKS * P
 
@@ -45,7 +47,7 @@ def tile_ka_attention_heads_mod_pa_kernel(tc, x, lin_w, lin_b, grid, coef, shift
 
     with ExitStack() as stack:
         keep = stack.enter_context(tc.tile_pool(name="keep", bufs=1))
-        psum_turn = stack.enter_context(tc.psum_pool(name="psum_turn", bufs=3))
+        psum_turn = stack.enter_context(tc.psum_pool(name="psum_turn", bufs=4))
         psum_acc = stack.enter_context(tc.psum_pool(name="psum_acc", bufs=2))
         psum_sums = stack.enter_context(tc.psum_pool(name="psum_sums", bufs=2))
 
@@ -139,6 +141,8 @@ def tile_ka_attention_heads_mod_pa_kernel(tc, x, lin_w, lin_b, grid, coef, shift
             quantise(w_grouped, w_codes, w_scales, W_BLOCKS * P)
 
         loop = stack.enter_context(tc.tile_pool(name="loop", bufs=2))
+        halves = GROUPS * FREQS * UNITS
+        halves_per_group = FREQS * UNITS
 
         def project(j):
             first_row = min((2 * SEG * j) // W_BLOCKS, WINDOW - ROWS)
@@ -180,22 +184,40 @@ def tile_ka_attention_heads_mod_pa_kernel(tc, x, lin_w, lin_b, grid, coef, shift
                 )
             return turned
 
-        def keep_coef(turned):
-            coef_t = loop.tile([P, UNIT], BF16, name="coef_t", bufs=COEF_AHEAD + 2)
-            nc.scalar.copy(out=coef_t[:], in_=turned[:])
-            return coef_t
 
-        def sines(i, xl_t, first_seg):
-            jm, unit = divmod(i, UNITS)
-            rate = turns[:, jm : jm + 1]
-            xl = xl_t[:, :, first_seg + unit * UNIT : first_seg + (unit + 1) * UNIT]
-            whole = loop.tile([P, BATCH, UNIT], I32, name="whole", bufs=1)
-            nc.vector.tensor_scalar(out=whole[:], in0=xl, scalar1=rate, scalar2=-0.25, op0=ALU.mult, op1=ALU.add)
+        def xl_of_half(i):
+            xl_t, first_seg = xl_of[i // halves_per_group][0:2]
+            unit = i % UNITS
+            return xl_t[:, :, first_seg + unit * UNIT : first_seg + (unit + 1) * UNIT]
+
+        def whole_turns(i):
+            whole = loop.tile([P, BATCH, UNIT], I32, name="whole", bufs=WHOLE_AHEAD + 1)
+            nc.gpsimd.tensor_scalar(
+                out=whole[:],
+                in0=xl_of_half(i),
+                scalar1=turns[:, i // UNITS : i // UNITS + 1],
+                scalar2=-0.25,
+                op0=ALU.mult,
+                op1=ALU.add,
+            )
+            return whole
+
+        def rest_of_turn(i, whole):
             rest = loop.tile([P, BATCH, UNIT], F32, name="rest", bufs=3)
             nc.vector.scalar_tensor_tensor(
-                out=rest[:], in0=xl, scalar=rate, in1=whole[:], op0=ALU.mult, op1=ALU.subtract
+                out=rest[:],
+                in0=xl_of_half(i),
+                scalar=turns[:, i // UNITS : i // UNITS + 1],
+                in1=whole[:],
+                op0=ALU.mult,
+                op1=ALU.subtract,
             )
+            return rest
+
+        def distance(rest):
             nc.scalar.activation(out=rest[:], in_=rest[:], func=ACT.Abs, bias=minus_quarter[:, 0:1])
+
+        def sine_of_distance(rest):
             sine = loop.tile([P, BATCH, UNIT], F32, name="sine", bufs=3)
             nc.scalar.activation(
                 out=sine[:], in_=rest[:], func=ACT.Sin, scale=-2.0 * math.pi, bias=quarter_turn[:, 0:1]
@@ -238,33 +260,34 @@ def tile_ka_attention_heads_mod_pa_kernel(tc, x, lin_w, lin_b, grid, coef, shift
             )
             nc.sync.dma_start(out=out_view[:, :, block, :], in_=total[:])
 
-        halves = GROUPS * FREQS * UNITS
-        halves_per_group = FREQS * UNITS
-        turned_of = {}
         coef_t_of = {}
+        whole_of = {}
+        rest_of = {}
         sine_of = {}
         products_of = {}
         sums_of = {}
         with tc.manual_schedule():
             xl_of = {0: project(0)}
-            for i in range(COEF_AHEAD):
-                turned_of[i] = turn_coef(i)
-                if i >= 1:
-                    coef_t_of[i - 1] = keep_coef(turned_of[i - 1])
-            for i in range(halves + 3):
-                j, local = divmod(i, halves_per_group)
+            for i in range(WHOLE_AHEAD):
+                whole_of[i] = whole_turns(i)
+            for i in range(halves + PRODUCT_LAG + STORE_LAG + 1):
+                if i + WHOLE_AHEAD < halves:
+                    whole_of[i + WHOLE_AHEAD] = whole_turns(i + WHOLE_AHEAD)
                 if i < halves:
-                    sine_of[i] = sines(i, xl_of[j][0], xl_of[j][1])
-                ahead = i + COEF_AHEAD
-                if ahead < halves:
-                    turned_of[ahead] = turn_coef(ahead)
-                if ahead - 1 < halves:
-                    coef_t_of[ahead - 1] = keep_coef(turned_of[ahead - 1])
+                    rest_of[i] = rest_of_turn(i, whole_of[i])
                 if 1 <= i <= halves:
-                    products_of[i - 1] = four_terms(sine_of[i - 1], coef_t_of[i - 1])
-                if i >= 2 and i % 2 == 0 and i <= halves:
-                    add_up((i - 2) // 2)
-                if i >= 3 and i % 2 == 1:
-                    store((i - 3) // 2)
+                    sine_of[i - 1] = sine_of_distance(rest_of[i - 1])
+                if i < halves:
+                    coef_t_of[i] = turn_coef(i)
+                    distance(rest_of[i])
+                multiplied = i - PRODUCT_LAG
+                if 0 <= multiplied < halves:
+                    products_of[multiplied] = four_terms(sine_of[multiplied], coef_t_of[multiplied])
+                stored = multiplied - STORE_LAG
+                if stored >= 0 and stored % 2 == 1:
+                    store(stored // 2)
+                if 0 <= multiplied < halves and multiplied % 2 == 1:
+                    add_up(multiplied // 2)
+                j, local = divmod(i, halves_per_group)
                 if j + 1 < GROUPS and local == halves_per_group // 2:
                     xl_of[j + 1] = project(j + 1)

@@ -29,7 +29,6 @@ WINDOW = 128
 WINDOW_STEP = 64
 ROWS = 78
 TERMS = 8
-WHOLE_AHEAD = 2
 PRODUCT_LAG = 2
 STORE_LAG = 2
 
@@ -191,8 +190,8 @@ def tile_ka_attention_heads_mod_pa_kernel(tc, x, lin_w, lin_b, grid, coef, shift
             return xl_t[:, :, first_seg + unit * UNIT : first_seg + (unit + 1) * UNIT]
 
         def whole_turns(i):
-            whole = loop.tile([P, BATCH, UNIT], I32, name="whole", bufs=WHOLE_AHEAD + 1)
-            nc.gpsimd.tensor_scalar(
+            whole = loop.tile([P, BATCH, UNIT], I32, name="whole")
+            nc.vector.tensor_scalar(
                 out=whole[:],
                 in0=xl_of_half(i),
                 scalar1=turns[:, i // UNITS : i // UNITS + 1],
@@ -268,11 +267,10 @@ def tile_ka_attention_heads_mod_pa_kernel(tc, x, lin_w, lin_b, grid, coef, shift
         sums_of = {}
         with tc.manual_schedule():
             xl_of = {0: project(0)}
-            for i in range(WHOLE_AHEAD):
-                whole_of[i] = whole_turns(i)
+            whole_of[0] = whole_turns(0)
             for i in range(halves + PRODUCT_LAG + STORE_LAG + 1):
-                if i + WHOLE_AHEAD < halves:
-                    whole_of[i + WHOLE_AHEAD] = whole_turns(i + WHOLE_AHEAD)
+                if i + 1 < halves:
+                    whole_of[i + 1] = whole_turns(i + 1)
                 if i < halves:
                     rest_of[i] = rest_of_turn(i, whole_of[i])
                 if 1 <= i <= halves:

import math
from contextlib import ExitStack

import concourse.mybir as mybir
from concourse.masks import make_identity

F32 = mybir.dt.float32
BF16 = mybir.dt.bfloat16
I32 = mybir.dt.int32
U32 = mybir.dt.uint32
U8 = mybir.dt.uint8
FP8X4 = mybir.dt.float8_e4m3fn_x4
ALU = mybir.AluOpType
ACT = mybir.ActivationFunctionType

P = 128
BATCH = 2
X_ROWS = 384
K = 512
W_BLOCKS = 20
GROUPS = 5
FREQS = 8
SEG = 128
TILES = 12
UNIT_TILES = 4
UNITS = TILES // UNIT_TILES
UNIT = UNIT_TILES * SEG
WINDOW = 128
WINDOW_STEP = 64
ROWS = 78
TERMS = 8
PRODUCT_LAG = 2
STORE_LAG = 2

FLOPS = 2 * BATCH * X_ROWS * K * W_BLOCKS * P


def tile_ka_attention_heads_mod_pa_kernel(tc, x, lin_w, lin_b, grid, coef, shift, out):
    nc = tc.nc

    x_view = x.rearrange("b h p k -> (b h p) k").rearrange("(a p) k -> p a k", p=P)
    w_view = lin_w.rearrange("(a p) k -> p a k", p=P)
    coef_view = coef.rearrange("(t q d) m j -> t q (d m j)", q=P, d=SEG)
    shift_view = shift.rearrange("o h g p (c d) -> (p c) (o h g) d", d=SEG)
    out_view = out.rearrange("b h g p (c d) -> (p c) b (h g) d", d=SEG)

    with ExitStack() as stack:
        keep = stack.enter_context(tc.tile_pool(name="keep", bufs=1))
        psum_turn = stack.enter_context(tc.psum_pool(name="psum_turn", bufs=4))
        psum_acc = stack.enter_context(tc.psum_pool(name="psum_acc", bufs=2))
        psum_sums = stack.enter_context(tc.psum_pool(name="psum_sums", bufs=2))

        x_tiles = BATCH * X_ROWS // P
        x_codes = keep.tile([P, x_tiles * P], U32, name="x_codes", align_bytes=64)
        x_scales = keep.tile([P, x_tiles * P], U8, name="x_scales", align_bytes=64)
        w_codes = keep.tile([P, W_BLOCKS * P], U32, name="w_codes", align_bytes=64)
        w_scales = keep.tile([P, W_BLOCKS * P], U8, name="w_scales", align_bytes=64)
        coef_sb = keep.tile([P, TILES * SEG, FREQS * GROUPS], BF16, name="coef_sb")
        ident = keep.tile([P, P], F32, name="ident")
        ident_bf = keep.tile([P, P], BF16, name="ident_bf")
        bias_t = keep.tile([P, W_BLOCKS], F32, name="bias_t")
        turns = keep.tile([P, GROUPS * FREQS], F32, name="turns")
        minus_quarter = keep.tile([P, 1], F32, name="minus_quarter")
        quarter_turn = keep.tile([P, 1], F32, name="quarter_turn")

        with tc.tile_pool(name="prep", bufs=1) as prep:
            x_raw = prep.tile([P, x_tiles * K], BF16, name="x_raw")
            w_raw = prep.tile([P, W_BLOCKS * K], BF16, name="w_raw")
            x_grouped = prep.tile([P, x_tiles * P * 4], BF16, name="x_grouped", align_bytes=64)
            w_grouped = prep.tile([P, W_BLOCKS * P * 4], BF16, name="w_grouped", align_bytes=64)
            bias_rows = prep.tile([P, P], BF16, name="bias_rows")
            bias_rows_f = prep.tile([P, P], F32, name="bias_rows_f")
            grid_bc = prep.tile([P, GROUPS * FREQS], BF16, name="grid_bc")

            nc.vector.memset(bias_rows[:], 0.0)
            nc.vector.memset(minus_quarter[:], -0.25)
            nc.vector.tensor_scalar(
                out=quarter_turn[:], in0=minus_quarter[:], scalar1=-2.0 * math.pi, scalar2=None, op0=ALU.mult
            )
            make_identity(nc, ident[:])
            make_identity(nc, ident_bf[:])

            nc.sync.dma_start(out=x_raw[:].rearrange("p (a k) -> p a k", k=K), in_=x_view)
            for c in range(GROUPS):
                nc.sync.dma_start(
                    out=w_raw[:, c * 4 * K : (c + 1) * 4 * K].rearrange("p (a k) -> p a k", k=K),
                    in_=w_view[:, c * 4 : (c + 1) * 4, :],
                )
            for t in range(TILES):
                nc.sync.dma_start(
                    out=coef_sb[:, t * SEG : (t + 1) * SEG, :].rearrange("p d c -> p (d c)"),
                    in_=coef_view[t],
                )
            nc.scalar.dma_start(out=bias_rows[0:W_BLOCKS, :], in_=lin_b.rearrange("(a d) -> a d", d=P))
            nc.scalar.dma_start(out=grid_bc[:], in_=grid.rearrange("j m -> (j m)").partition_broadcast(P))

            nc.vector.tensor_scalar(
                out=turns[:], in0=grid_bc[:], scalar1=1.0 / (2.0 * math.pi), scalar2=None, op0=ALU.mult
            )

            nc.vector.tensor_copy(out=bias_rows_f[:], in_=bias_rows[:])
            bias_ps = psum_acc.tile([P, UNIT], F32, name="bias_ps", tag="acc")
            nc.tensor.transpose(bias_ps[:, 0:P], bias_rows_f[:], ident[:])
            nc.vector.tensor_copy(out=bias_t[:], in_=bias_ps[:, 0:W_BLOCKS])

            def put_k_on_partitions(raw, grouped, n_tiles):
                words = raw[:].bitcast(F32)
                grouped_words = grouped[:].bitcast(F32)
                for pair in range(n_tiles // 2):
                    bank = psum_turn.tile([P, UNIT], F32, name="turned", tag="bank")
                    for a in range(2):
                        for u in range(2):
                            first = ((pair * 2 + a) * 2 + u) * P
                            nc.tensor.transpose(
                                bank[:, (a * 2 + u) * P : (a * 2 + u + 1) * P],
                                words[:, first : first + P],
                                ident[:],
                            )
                    dst = grouped_words[:, pair * UNIT : (pair + 1) * UNIT].rearrange(
                        "p (a r u) -> p a r u", a=2, u=2
                    )
                    src = bank[:].rearrange("p (a u r) -> p a r u", a=2, u=2)
                    if pair % 2 == 0:
                        nc.vector.tensor_copy(out=dst, in_=src)
                    else:
                        nc.scalar.copy(out=dst, in_=src)

            def quantise(grouped, codes, scales, n_rows):
                for first in range(0, n_rows, 512):
                    n = min(512, n_rows - first)
                    nc.vector.quantize_mx(
                        out=codes[:, first : first + n].bitcast(FP8X4),
                        scales=scales[:, first : first + n],
                        in_=grouped[:, first * 4 : (first + n) * 4],
                    )

            put_k_on_partitions(x_raw, x_grouped, x_tiles)
            put_k_on_partitions(w_raw, w_grouped, W_BLOCKS)
            quantise(x_grouped, x_codes, x_scales, x_tiles * P)
            quantise(w_grouped, w_codes, w_scales, W_BLOCKS * P)

        loop = stack.enter_context(tc.tile_pool(name="loop", bufs=2))
        halves = GROUPS * FREQS * UNITS
        halves_per_group = FREQS * UNITS

        def project(j):
            first_row = min((2 * SEG * j) // W_BLOCKS, WINDOW - ROWS)
            shift_sb = loop.tile([P, TILES, SEG], BF16, name="shift_sb")
            nc.sync.dma_start(out=shift_sb[:], in_=shift_view[:, j * TILES : (j + 1) * TILES, :])
            xl_t = loop.tile([P, BATCH, ROWS * W_BLOCKS], F32, name="xl_t")
            for b in range(BATCH):
                window = b * X_ROWS + WINDOW_STEP * j
                for c in range(GROUPS):
                    acc = psum_acc.tile([P, UNIT], F32, name="acc", tag="acc")
                    for d in range(4):
                        a = c * 4 + d
                        nc.tensor.matmul_mx(
                            out=acc[:, d * WINDOW : (d + 1) * WINDOW],
                            lhsT=w_codes[:, a * P : (a + 1) * P].bitcast(FP8X4),
                            lhsT_scale=w_scales[:, a * P : (a + 1) * P],
                            rhs=x_codes[:, window : window + WINDOW].bitcast(FP8X4),
                            rhs_scale=x_scales[:, window : window + WINDOW],
                            start=True,
                            stop=True,
                        )
                    nc.vector.tensor_tensor(
                        out=xl_t[:, b, :].rearrange("p (r a) -> p r a", a=W_BLOCKS)[:, :, c * 4 : (c + 1) * 4],
                        in0=acc[:].rearrange("p (d r) -> p r d", d=4)[:, first_row : first_row + ROWS, :],
                        in1=bias_t[:, c * 4 : (c + 1) * 4].unsqueeze(1).to_broadcast([P, ROWS, 4]),
                        op=ALU.add,
                    )
            return xl_t, 2 * SEG * j - W_BLOCKS * first_row, shift_sb

        def turn_coef(i):
            jm, unit = divmod(i, UNITS)
            j, m = divmod(jm, FREQS)
            column = m * GROUPS + j
            turned = psum_turn.tile([P, UNIT], BF16, name="coef_ps", tag="bank")
            for t in range(UNIT_TILES):
                first = (unit * UNIT_TILES + t) * SEG
                nc.tensor.transpose(
                    turned[:, t * SEG : (t + 1) * SEG], coef_sb[:, first : first + SEG, column], ident_bf[:]
                )
            return turned


        def xl_of_half(i):
            xl_t, first_seg = xl_of[i // halves_per_group][0:2]
            unit = i % UNITS
            return xl_t[:, :, first_seg + unit * UNIT : first_seg + (unit + 1) * UNIT]

        def whole_turns(i):
            whole = loop.tile([P, BATCH, UNIT], I32, name="whole")
            nc.vector.tensor_scalar(
                out=whole[:],
                in0=xl_of_half(i),
                scalar1=turns[:, i // UNITS : i // UNITS + 1],
                scalar2=-0.25,
                op0=ALU.mult,
                op1=ALU.add,
            )
            return whole

        def rest_of_turn(i, whole):
            rest = loop.tile([P, BATCH, UNIT], F32, name="rest", bufs=3)
            nc.vector.scalar_tensor_tensor(
                out=rest[:],
                in0=xl_of_half(i),
                scalar=turns[:, i // UNITS : i // UNITS + 1],
                in1=whole[:],
                op0=ALU.mult,
                op1=ALU.subtract,
            )
            return rest

        def distance(rest):
            nc.scalar.activation(out=rest[:], in_=rest[:], func=ACT.Abs, bias=minus_quarter[:, 0:1])

        def sine_of_distance(rest):
            sine = loop.tile([P, BATCH, UNIT], F32, name="sine", bufs=3)
            nc.scalar.activation(
                out=sine[:], in_=rest[:], func=ACT.Sin, scale=-2.0 * math.pi, bias=quarter_turn[:, 0:1]
            )
            return sine

        def four_terms(sine, coef_t):
            products = loop.tile([P, BATCH, UNIT], F32, name="products", bufs=5)
            nc.vector.tensor_tensor(
                out=products[:],
                in0=sine[:],
                in1=coef_t[:].unsqueeze(1).to_broadcast([P, BATCH, UNIT]),
                op=ALU.mult,
            )
            return products

        def add_up(block):
            sums = psum_sums.tile([P, BATCH, SEG], F32, name="sums")
            for b in range(BATCH):
                for e in range(TERMS):
                    products = products_of[2 * block + e // UNIT_TILES]
                    t = e % UNIT_TILES
                    nc.tensor.matmul(
                        out=sums[:, b, :],
                        lhsT=products[:, b, t * SEG : (t + 1) * SEG],
                        rhs=ident[:],
                        is_transpose=True,
                        start=(e == 0),
                        stop=(e == TERMS - 1),
                    )
            sums_of[block] = sums

        def store(block):
            total = loop.tile([P, BATCH, SEG], F32, name="total")
            nc.vector.tensor_tensor(
                out=total[:],
                in0=sums_of[block][:],
                in1=xl_of[block // TILES][2][:, block % TILES : block % TILES + 1, :].to_broadcast([P, BATCH, SEG]),
                op=ALU.add,
            )
            nc.sync.dma_start(out=out_view[:, :, block, :], in_=total[:])

        coef_t_of = {}
        whole_of = {}
        rest_of = {}
        sine_of = {}
        products_of = {}
        sums_of = {}
        with tc.manual_schedule():
            xl_of = {0: project(0)}
            whole_of[0] = whole_turns(0)
            for i in range(halves + PRODUCT_LAG + STORE_LAG + 1):
                if i + 1 < halves:
                    whole_of[i + 1] = whole_turns(i + 1)
                if i < halves:
                    rest_of[i] = rest_of_turn(i, whole_of[i])
                if 1 <= i <= halves:
                    sine_of[i - 1] = sine_of_distance(rest_of[i - 1])
                if i < halves:
                    coef_t_of[i] = turn_coef(i)
                    distance(rest_of[i])
                multiplied = i - PRODUCT_LAG
                if 0 <= multiplied < halves:
                    products_of[multiplied] = four_terms(sine_of[multiplied], coef_t_of[multiplied])
                stored = multiplied - STORE_LAG
                if stored >= 0 and stored % 2 == 1:
                    store(stored // 2)
                if 0 <= multiplied < halves and multiplied % 2 == 1:
                    add_up(multiplied // 2)
                j, local = divmod(i, halves_per_group)
                if j + 1 < GROUPS and local == halves_per_group // 2:
                    xl_of[j + 1] = project(j + 1)
